import numpy as np
import ml_dtypes

BF16 = ml_dtypes.bfloat16


def bf(x):
    return np.asarray(x, np.float32).astype(BF16)


def f32(x):
    return np.asarray(x, np.float32)


def f64(x):
    return np.asarray(x).astype(np.float64)


def striped(idx):
    return np.tile(idx.reshape(-1, 16).T, (8, 1))


K, S, N, D = 512, 1024, 512, 256


def setup_inputs():
    return {"base": f32(8.0 + np.random.standard_normal((K, S))), "x": bf(2.0 * np.random.standard_normal((D, N)) / np.sqrt(D)), "cent": bf(2.0 * np.random.standard_normal((K, D)) / np.sqrt(D)), "offs": striped(np.random.permutation(S)[:N])}


def reference(base, x, cent, offs):
    idx = offs[:16].T.reshape(-1)
    x, cent = f64(x), f64(cent)
    x2 = np.sum(x * x, axis=0, keepdims=True)
    c2 = np.sum(cent * cent, axis=1, keepdims=True)
    xc = cent @ x
    out = f64(base).copy()
    out[:, idx] = (c2 - 2.0 * xc) + x2
    return out

@@ -1,0 +1,70 @@
+import concourse.mybir as mybir
+from concourse.masks import make_identity
+
+P = 128
+K, S, N, D = 512, 1024, 512, 256
+K_BLOCKS = K // P
+D_CHUNKS = D // P
+
+FLOPS = 2 * K * N * D
+
+BF16, F32, U16 = mybir.dt.bfloat16, mybir.dt.float32, mybir.dt.uint16
+ADD, MULT = mybir.AluOpType.add, mybir.AluOpType.mult
+ACT = mybir.ActivationFunctionType
+
+
+def tile_losskmeans_kernel(tc, base, x, cent, offs, out):
+    nc = tc.nc
+    with (
+        tc.tile_pool(name="held", bufs=1) as held,
+        tc.tile_pool(name="work", bufs=2) as work,
+        tc.psum_pool(name="psum", bufs=2) as psum,
+    ):
+        offsets = held.tile([P, N // 16], U16, name="offsets")
+        nc.sync.dma_start(offsets[:], offs)
+
+        x_sb = held.tile([P, D_CHUNKS, N], BF16, name="x_sb")
+        nc.scalar.dma_start(x_sb[:], x.rearrange("(c p) n -> p c n", p=P))
+        cent_sb = held.tile([P, K_BLOCKS, D], BF16, name="cent_sb")
+        nc.scalar.dma_start(cent_sb[:], cent.rearrange("(b p) d -> p b d", p=P))
+
+        windows = []
+        for b in range(K_BLOCKS):
+            window = held.tile([P, S], F32, name=f"window{b}")
+            nc.sync.dma_start(window[:], base[b * P : (b + 1) * P, :])
+            windows.append(window)
+
+        identity = held.tile([P, P], BF16, name="identity")
+        make_identity(nc, identity[:])
+        ones = held.tile([P, P], BF16, name="ones")
+        nc.gpsimd.memset(ones[:], 1.0)
+
+        x_squared = held.tile([P, D_CHUNKS, N], BF16, name="x_squared")
+        nc.vector.tensor_tensor(x_squared[:], x_sb[:], x_sb[:], MULT)
+        x2_psum = psum.tile([P, N], F32, name="x2_psum")
+        for c in range(D_CHUNKS):
+            nc.tensor.matmul(x2_psum[:], ones[:], x_squared[:, c, :], start=(c == 0), stop=(c == D_CHUNKS - 1))
+        x2_rows = held.tile([P, N], F32, name="x2_rows")
+        nc.vector.tensor_copy(x2_rows[:], x2_psum[:])
+
+        c2 = held.tile([P, K_BLOCKS], F32, name="c2")
+
+        for b in range(K_BLOCKS):
+            cent_squared = work.tile([P, D], F32, name="cent_squared")
+            nc.scalar.activation(cent_squared[:], cent_sb[:, b, :], ACT.Square, accum_out=c2[:, b : b + 1])
+
+            centT_psum = psum.tile([P, D_CHUNKS, P], BF16, name="centT_psum")
+            for c in range(D_CHUNKS):
+                nc.tensor.transpose(centT_psum[:, c, :], cent_sb[:, b, c * P : (c + 1) * P], identity[:])
+            centT = work.tile([P, D_CHUNKS, P], BF16, name="centT")
+            nc.scalar.activation(centT[:], centT_psum[:], ACT.Copy)
+
+            xc_psum = psum.tile([P, N], F32, name="xc_psum")
+            for c in range(D_CHUNKS):
+                nc.tensor.matmul(xc_psum[:], centT[:, c, :], x_sb[:, c, :], start=(c == 0), stop=(c == D_CHUNKS - 1))
+
+            c2_minus_2xc = work.tile([P, N], F32, name="c2_minus_2xc")
+            nc.scalar.activation(c2_minus_2xc[:], xc_psum[:], ACT.Identity, bias=c2[:, b : b + 1], scale=-2.0)
+
+            nc.vector.tensor_tensor(windows[b][:].indirect(offsets[:]), c2_minus_2xc[:], x2_rows[:], ADD)
+            nc.sync.dma_start(out[b * P : (b + 1) * P, :], windows[b][:])

@@ -20,24 +20,38 @@ def tile_losskmeans_kernel(tc, base, x, cent, offs, out):
         tc.tile_pool(name="work", bufs=2) as work,
         tc.psum_pool(name="psum", bufs=2) as psum,
     ):
+        x_sb = held.tile([P, D_CHUNKS, N], BF16, name="x_sb")
+        nc.scalar.dma_start(x_sb[:], x.rearrange("(c p) n -> p c n", p=P))
+
         offsets = held.tile([P, N // 16], U16, name="offsets")
         nc.sync.dma_start(offsets[:], offs)
 
-        x_sb = held.tile([P, D_CHUNKS, N], BF16, name="x_sb")
-        nc.scalar.dma_start(x_sb[:], x.rearrange("(c p) n -> p c n", p=P))
-        cent_sb = held.tile([P, K_BLOCKS, D], BF16, name="cent_sb")
-        nc.scalar.dma_start(cent_sb[:], cent.rearrange("(b p) d -> p b d", p=P))
-
+        cent_rows = []
         windows = []
         for b in range(K_BLOCKS):
-            window = held.tile([P, S], F32, name=f"window{b}")
-            nc.sync.dma_start(window[:], base[b * P : (b + 1) * P, :])
-            windows.append(window)
+            cent_rows.append(held.tile([P, D], BF16, name=f"cent_rows{b}"))
+            nc.sync.dma_start(cent_rows[b][:], cent[b * P : (b + 1) * P, :])
+            windows.append(held.tile([P, S], F32, name=f"window{b}"))
+            nc.sync.dma_start(windows[b][:], base[b * P : (b + 1) * P, :])
 
         identity = held.tile([P, P], BF16, name="identity")
         make_identity(nc, identity[:])
         ones = held.tile([P, P], BF16, name="ones")
         nc.gpsimd.memset(ones[:], 1.0)
+
+        c2 = held.tile([P, K_BLOCKS], F32, name="c2")
+        centT = []
+
+        def prepare_centroids(b):
+            cent_squared = work.tile([P, D], F32, name="cent_squared")
+            nc.scalar.activation(cent_squared[:], cent_rows[b][:], ACT.Square, accum_out=c2[:, b : b + 1])
+            centT_psum = psum.tile([P, D_CHUNKS, P], BF16, name="centT_psum")
+            for c in range(D_CHUNKS):
+                nc.tensor.transpose(centT_psum[:, c, :], cent_rows[b][:, c * P : (c + 1) * P], identity[:])
+            centT.append(held.tile([P, D_CHUNKS, P], BF16, name=f"centT{b}"))
+            nc.scalar.activation(centT[b][:], centT_psum[:], ACT.Copy)
+
+        prepare_centroids(0)
 
         x_squared = held.tile([P, D_CHUNKS, N], BF16, name="x_squared")
         nc.vector.tensor_tensor(x_squared[:], x_sb[:], x_sb[:], MULT)
@@ -47,24 +61,16 @@ def tile_losskmeans_kernel(tc, base, x, cent, offs, out):
         x2_rows = held.tile([P, N], F32, name="x2_rows")
         nc.vector.tensor_copy(x2_rows[:], x2_psum[:])
 
-        c2 = held.tile([P, K_BLOCKS], F32, name="c2")
-
         for b in range(K_BLOCKS):
-            cent_squared = work.tile([P, D], F32, name="cent_squared")
-            nc.scalar.activation(cent_squared[:], cent_sb[:, b, :], ACT.Square, accum_out=c2[:, b : b + 1])
-
-            centT_psum = psum.tile([P, D_CHUNKS, P], BF16, name="centT_psum")
-            for c in range(D_CHUNKS):
-                nc.tensor.transpose(centT_psum[:, c, :], cent_sb[:, b, c * P : (c + 1) * P], identity[:])
-            centT = work.tile([P, D_CHUNKS, P], BF16, name="centT")
-            nc.scalar.activation(centT[:], centT_psum[:], ACT.Copy)
-
             xc_psum = psum.tile([P, N], F32, name="xc_psum")
             for c in range(D_CHUNKS):
-                nc.tensor.matmul(xc_psum[:], centT[:, c, :], x_sb[:, c, :], start=(c == 0), stop=(c == D_CHUNKS - 1))
+                nc.tensor.matmul(xc_psum[:], centT[b][:, c, :], x_sb[:, c, :], start=(c == 0), stop=(c == D_CHUNKS - 1))
 
             c2_minus_2xc = work.tile([P, N], F32, name="c2_minus_2xc")
             nc.scalar.activation(c2_minus_2xc[:], xc_psum[:], ACT.Identity, bias=c2[:, b : b + 1], scale=-2.0)
+
+            if b + 1 < K_BLOCKS:
+                prepare_centroids(b + 1)
 
             nc.vector.tensor_tensor(windows[b][:].indirect(offsets[:]), c2_minus_2xc[:], x2_rows[:], ADD)
             nc.sync.dma_start(out[b * P : (b + 1) * P, :], windows[b][:])

@@ -8,6 +8,8 @@ D_CHUNKS = D // P
 
 FLOPS = 2 * K * N * D
 
+WARM_MATMULS = 5
+
 BF16, F32, U16 = mybir.dt.bfloat16, mybir.dt.float32, mybir.dt.uint16
 ADD, MULT = mybir.AluOpType.add, mybir.AluOpType.mult
 ACT = mybir.ActivationFunctionType
@@ -20,36 +22,37 @@ def tile_losskmeans_kernel(tc, base, x, cent, offs, out):
         tc.tile_pool(name="work", bufs=2) as work,
         tc.psum_pool(name="psum", bufs=2) as psum,
     ):
+        cent_sb = held.tile([P, K_BLOCKS, D], BF16, name="cent_sb")
+        nc.scalar.dma_start(cent_sb[:], cent.rearrange("(b p) d -> p b d", p=P))
         x_sb = held.tile([P, D_CHUNKS, N], BF16, name="x_sb")
-        nc.scalar.dma_start(x_sb[:], x.rearrange("(c p) n -> p c n", p=P))
-
+        nc.sync.dma_start(x_sb[:], x.rearrange("(c p) n -> p c n", p=P))
         offsets = held.tile([P, N // 16], U16, name="offsets")
         nc.sync.dma_start(offsets[:], offs)
-
-        cent_rows = []
         windows = []
         for b in range(K_BLOCKS):
-            cent_rows.append(held.tile([P, D], BF16, name=f"cent_rows{b}"))
-            nc.sync.dma_start(cent_rows[b][:], cent[b * P : (b + 1) * P, :])
             windows.append(held.tile([P, S], F32, name=f"window{b}"))
             nc.sync.dma_start(windows[b][:], base[b * P : (b + 1) * P, :])
 
+        ones = held.tile([P, N], BF16, name="ones")
+        nc.gpsimd.memset(ones[:], 1.0)
         identity = held.tile([P, P], BF16, name="identity")
         make_identity(nc, identity[:])
-        ones = held.tile([P, P], BF16, name="ones")
-        nc.gpsimd.memset(ones[:], 1.0)
+
+        warm_psum = psum.tile([P, N], F32, name="warm_psum")
+        for i in range(WARM_MATMULS):
+            nc.tensor.matmul(warm_psum[:], ones[:, :P], ones[:], start=True, stop=True)
 
         c2 = held.tile([P, K_BLOCKS], F32, name="c2")
         centT = []
 
         def prepare_centroids(b):
-            cent_squared = work.tile([P, D], F32, name="cent_squared")
-            nc.scalar.activation(cent_squared[:], cent_rows[b][:], ACT.Square, accum_out=c2[:, b : b + 1])
             centT_psum = psum.tile([P, D_CHUNKS, P], BF16, name="centT_psum")
             for c in range(D_CHUNKS):
-                nc.tensor.transpose(centT_psum[:, c, :], cent_rows[b][:, c * P : (c + 1) * P], identity[:])
+                nc.tensor.transpose(centT_psum[:, c, :], cent_sb[:, b, c * P : (c + 1) * P], identity[:])
             centT.append(held.tile([P, D_CHUNKS, P], BF16, name=f"centT{b}"))
             nc.scalar.activation(centT[b][:], centT_psum[:], ACT.Copy)
+            cent_squared = work.tile([P, D], F32, name="cent_squared")
+            nc.scalar.activation(cent_squared[:], cent_sb[:, b, :], ACT.Square, accum_out=c2[:, b : b + 1])
 
         prepare_centroids(0)
 
@@ -57,7 +60,7 @@ def tile_losskmeans_kernel(tc, base, x, cent, offs, out):
         nc.vector.tensor_tensor(x_squared[:], x_sb[:], x_sb[:], MULT)
         x2_psum = psum.tile([P, N], F32, name="x2_psum")
         for c in range(D_CHUNKS):
-            nc.tensor.matmul(x2_psum[:], ones[:], x_squared[:, c, :], start=(c == 0), stop=(c == D_CHUNKS - 1))
+            nc.tensor.matmul(x2_psum[:], ones[:, :P], x_squared[:, c, :], start=(c == 0), stop=(c == D_CHUNKS - 1))
         x2_rows = held.tile([P, N], F32, name="x2_rows")
         nc.vector.tensor_copy(x2_rows[:], x2_psum[:])
 

@@ -34,7 +34,7 @@ def tile_losskmeans_kernel(tc, base, x, cent, offs, out):
             nc.sync.dma_start(windows[b][:], base[b * P : (b + 1) * P, :])
 
         ones = held.tile([P, N], BF16, name="ones")
-        nc.gpsimd.memset(ones[:], 1.0)
+        nc.vector.memset(ones[:], 1.0)
         identity = held.tile([P, P], BF16, name="identity")
         make_identity(nc, identity[:])
 
@@ -43,37 +43,33 @@ def tile_losskmeans_kernel(tc, base, x, cent, offs, out):
             nc.tensor.matmul(warm_psum[:], ones[:, :P], ones[:], start=True, stop=True)
 
         c2 = held.tile([P, K_BLOCKS], F32, name="c2")
-        centT = []
-
-        def prepare_centroids(b):
+        c2_minus_2xc = []
+        for b in range(K_BLOCKS):
             centT_psum = psum.tile([P, D_CHUNKS, P], BF16, name="centT_psum")
             for c in range(D_CHUNKS):
                 nc.tensor.transpose(centT_psum[:, c, :], cent_sb[:, b, c * P : (c + 1) * P], identity[:])
-            centT.append(held.tile([P, D_CHUNKS, P], BF16, name=f"centT{b}"))
-            nc.scalar.activation(centT[b][:], centT_psum[:], ACT.Copy)
+            centT = work.tile([P, D_CHUNKS, P], BF16, name="centT")
+            nc.vector.tensor_copy(centT[:], centT_psum[:])
             cent_squared = work.tile([P, D], F32, name="cent_squared")
             nc.scalar.activation(cent_squared[:], cent_sb[:, b, :], ACT.Square, accum_out=c2[:, b : b + 1])
 
-        prepare_centroids(0)
-
-        x_squared = held.tile([P, D_CHUNKS, N], BF16, name="x_squared")
-        nc.vector.tensor_tensor(x_squared[:], x_sb[:], x_sb[:], MULT)
-        x2_psum = psum.tile([P, N], F32, name="x2_psum")
-        for c in range(D_CHUNKS):
-            nc.tensor.matmul(x2_psum[:], ones[:, :P], x_squared[:, c, :], start=(c == 0), stop=(c == D_CHUNKS - 1))
-        x2_rows = held.tile([P, N], F32, name="x2_rows")
-        nc.vector.tensor_copy(x2_rows[:], x2_psum[:])
-
-        for b in range(K_BLOCKS):
             xc_psum = psum.tile([P, N], F32, name="xc_psum")
             for c in range(D_CHUNKS):
-                nc.tensor.matmul(xc_psum[:], centT[b][:, c, :], x_sb[:, c, :], start=(c == 0), stop=(c == D_CHUNKS - 1))
+                nc.tensor.matmul(xc_psum[:], centT[:, c, :], x_sb[:, c, :], start=(c == 0), stop=(c == D_CHUNKS - 1))
+            c2_minus_2xc.append(held.tile([P, N], F32, name=f"c2_minus_2xc{b}"))
+            nc.scalar.activation(c2_minus_2xc[b][:], xc_psum[:], ACT.Identity, bias=c2[:, b : b + 1], scale=-2.0)
 
-            c2_minus_2xc = work.tile([P, N], F32, name="c2_minus_2xc")
-            nc.scalar.activation(c2_minus_2xc[:], xc_psum[:], ACT.Identity, bias=c2[:, b : b + 1], scale=-2.0)
+            if b == 0:
+                x_squared = held.tile([P, D_CHUNKS, N], BF16, name="x_squared")
+                nc.vector.tensor_tensor(x_squared[:], x_sb[:], x_sb[:], MULT)
+                x2_psum = psum.tile([P, N], F32, name="x2_psum")
+                for c in range(D_CHUNKS):
+                    nc.tensor.matmul(
+                        x2_psum[:], ones[:, :P], x_squared[:, c, :], start=(c == 0), stop=(c == D_CHUNKS - 1)
+                    )
+                x2_rows = held.tile([P, N], F32, name="x2_rows")
+                nc.vector.tensor_copy(x2_rows[:], x2_psum[:])
 
-            if b + 1 < K_BLOCKS:
-                prepare_centroids(b + 1)
-
-            nc.vector.tensor_tensor(windows[b][:].indirect(offsets[:]), c2_minus_2xc[:], x2_rows[:], ADD)
+        for b in range(K_BLOCKS):
+            nc.vector.tensor_tensor(windows[b][:].indirect(offsets[:]), c2_minus_2xc[b][:], x2_rows[:], ADD)
             nc.sync.dma_start(out[b * P : (b + 1) * P, :], windows[b][:])

@@ -43,33 +43,37 @@ def tile_losskmeans_kernel(tc, base, x, cent, offs, out):
             nc.tensor.matmul(warm_psum[:], ones[:, :P], ones[:], start=True, stop=True)
 
         c2 = held.tile([P, K_BLOCKS], F32, name="c2")
-        c2_minus_2xc = []
-        for b in range(K_BLOCKS):
+        centT = []
+
+        def prepare_centroids(b):
             centT_psum = psum.tile([P, D_CHUNKS, P], BF16, name="centT_psum")
             for c in range(D_CHUNKS):
                 nc.tensor.transpose(centT_psum[:, c, :], cent_sb[:, b, c * P : (c + 1) * P], identity[:])
-            centT = work.tile([P, D_CHUNKS, P], BF16, name="centT")
-            nc.vector.tensor_copy(centT[:], centT_psum[:])
+            centT.append(held.tile([P, D_CHUNKS, P], BF16, name=f"centT{b}"))
+            nc.scalar.activation(centT[b][:], centT_psum[:], ACT.Copy)
             cent_squared = work.tile([P, D], F32, name="cent_squared")
             nc.scalar.activation(cent_squared[:], cent_sb[:, b, :], ACT.Square, accum_out=c2[:, b : b + 1])
 
-            xc_psum = psum.tile([P, N], F32, name="xc_psum")
-            for c in range(D_CHUNKS):
-                nc.tensor.matmul(xc_psum[:], centT[:, c, :], x_sb[:, c, :], start=(c == 0), stop=(c == D_CHUNKS - 1))
-            c2_minus_2xc.append(held.tile([P, N], F32, name=f"c2_minus_2xc{b}"))
-            nc.scalar.activation(c2_minus_2xc[b][:], xc_psum[:], ACT.Identity, bias=c2[:, b : b + 1], scale=-2.0)
+        prepare_centroids(0)
 
-            if b == 0:
-                x_squared = held.tile([P, D_CHUNKS, N], BF16, name="x_squared")
-                nc.vector.tensor_tensor(x_squared[:], x_sb[:], x_sb[:], MULT)
-                x2_psum = psum.tile([P, N], F32, name="x2_psum")
-                for c in range(D_CHUNKS):
-                    nc.tensor.matmul(
-                        x2_psum[:], ones[:, :P], x_squared[:, c, :], start=(c == 0), stop=(c == D_CHUNKS - 1)
-                    )
-                x2_rows = held.tile([P, N], F32, name="x2_rows")
-                nc.vector.tensor_copy(x2_rows[:], x2_psum[:])
+        x_squared = held.tile([P, D_CHUNKS, N], BF16, name="x_squared")
+        nc.vector.tensor_tensor(x_squared[:], x_sb[:], x_sb[:], MULT)
+        x2_psum = psum.tile([P, N], F32, name="x2_psum")
+        for c in range(D_CHUNKS):
+            nc.tensor.matmul(x2_psum[:], ones[:, :P], x_squared[:, c, :], start=(c == 0), stop=(c == D_CHUNKS - 1))
+        x2_rows = held.tile([P, N], F32, name="x2_rows")
+        nc.vector.tensor_copy(x2_rows[:], x2_psum[:])
 
         for b in range(K_BLOCKS):
-            nc.vector.tensor_tensor(windows[b][:].indirect(offsets[:]), c2_minus_2xc[b][:], x2_rows[:], ADD)
+            xc_psum = psum.tile([P, N], F32, name="xc_psum")
+            for c in range(D_CHUNKS):
+                nc.tensor.matmul(xc_psum[:], centT[b][:, c, :], x_sb[:, c, :], start=(c == 0), stop=(c == D_CHUNKS - 1))
+
+            c2_minus_2xc = work.tile([P, N], F32, name="c2_minus_2xc")
+            nc.scalar.activation(c2_minus_2xc[:], xc_psum[:], ACT.Identity, bias=c2[:, b : b + 1], scale=-2.0)
+
+            if b + 1 < K_BLOCKS:
+                prepare_centroids(b + 1)
+
+            nc.vector.tensor_tensor(windows[b][:].indirect(offsets[:]), c2_minus_2xc[:], x2_rows[:], ADD)
             nc.sync.dma_start(out[b * P : (b + 1) * P, :], windows[b][:])

@@ -8,7 +8,7 @@ D_CHUNKS = D // P
 
 FLOPS = 2 * K * N * D
 
-WARM_MATMULS = 5
+WARM_MATMULS = 4
 
 BF16, F32, U16 = mybir.dt.bfloat16, mybir.dt.float32, mybir.dt.uint16
 ADD, MULT = mybir.AluOpType.add, mybir.AluOpType.mult
@@ -57,9 +57,9 @@ def tile_losskmeans_kernel(tc, base, x, cent, offs, out):
         prepare_centroids(0)
 
         x_squared = held.tile([P, D_CHUNKS, N], BF16, name="x_squared")
-        nc.vector.tensor_tensor(x_squared[:], x_sb[:], x_sb[:], MULT)
         x2_psum = psum.tile([P, N], F32, name="x2_psum")
         for c in range(D_CHUNKS):
+            nc.vector.tensor_tensor(x_squared[:, c, :], x_sb[:, c, :], x_sb[:, c, :], MULT)
             nc.tensor.matmul(x2_psum[:], ones[:, :P], x_squared[:, c, :], start=(c == 0), stop=(c == D_CHUNKS - 1))
         x2_rows = held.tile([P, N], F32, name="x2_rows")
         nc.vector.tensor_copy(x2_rows[:], x2_psum[:])

@@ -22,8 +22,8 @@ def tile_losskmeans_kernel(tc, base, x, cent, offs, out):
         tc.tile_pool(name="work", bufs=2) as work,
         tc.psum_pool(name="psum", bufs=2) as psum,
     ):
-        cent_sb = held.tile([P, K_BLOCKS, D], BF16, name="cent_sb")
-        nc.scalar.dma_start(cent_sb[:], cent.rearrange("(b p) d -> p b d", p=P))
+        cent_first = held.tile([P, D], BF16, name="cent_first")
+        nc.scalar.dma_start(cent_first[:], cent[0:P, :])
         x_sb = held.tile([P, D_CHUNKS, N], BF16, name="x_sb")
         nc.sync.dma_start(x_sb[:], x.rearrange("(c p) n -> p c n", p=P))
         offsets = held.tile([P, N // 16], U16, name="offsets")
@@ -31,16 +31,21 @@ def tile_losskmeans_kernel(tc, base, x, cent, offs, out):
         windows = []
         for b in range(K_BLOCKS):
             windows.append(held.tile([P, S], F32, name=f"window{b}"))
+        nc.sync.dma_start(windows[0][:], base[0:P, :])
+        cent_rest = held.tile([P, K_BLOCKS - 1, D], BF16, name="cent_rest")
+        nc.scalar.dma_start(cent_rest[:], cent[P:K, :].rearrange("(b p) d -> p b d", p=P))
+        for b in range(1, K_BLOCKS):
             nc.sync.dma_start(windows[b][:], base[b * P : (b + 1) * P, :])
+        cent_sb = [cent_first[:]] + [cent_rest[:, b - 1, :] for b in range(1, K_BLOCKS)]
 
-        ones = held.tile([P, N], BF16, name="ones")
+        ones = held.tile([P, P], BF16, name="ones")
         nc.vector.memset(ones[:], 1.0)
         identity = held.tile([P, P], BF16, name="identity")
         make_identity(nc, identity[:])
 
         warm_psum = psum.tile([P, N], F32, name="warm_psum")
         for i in range(WARM_MATMULS):
-            nc.tensor.matmul(warm_psum[:], ones[:, :P], ones[:], start=True, stop=True)
+            nc.tensor.matmul(warm_psum[:], ones[:], ones[:, 0:1].to_broadcast([P, N]), start=True, stop=True)
 
         c2 = held.tile([P, K_BLOCKS], F32, name="c2")
         centT = []
@@ -48,11 +53,11 @@ def tile_losskmeans_kernel(tc, base, x, cent, offs, out):
         def prepare_centroids(b):
             centT_psum = psum.tile([P, D_CHUNKS, P], BF16, name="centT_psum")
             for c in range(D_CHUNKS):
-                nc.tensor.transpose(centT_psum[:, c, :], cent_sb[:, b, c * P : (c + 1) * P], identity[:])
+                nc.tensor.transpose(centT_psum[:, c, :], cent_sb[b][:, c * P : (c + 1) * P], identity[:])
             centT.append(held.tile([P, D_CHUNKS, P], BF16, name=f"centT{b}"))
             nc.scalar.activation(centT[b][:], centT_psum[:], ACT.Copy)
             cent_squared = work.tile([P, D], F32, name="cent_squared")
-            nc.scalar.activation(cent_squared[:], cent_sb[:, b, :], ACT.Square, accum_out=c2[:, b : b + 1])
+            nc.scalar.activation(cent_squared[:], cent_sb[b], ACT.Square, accum_out=c2[:, b : b + 1])
 
         prepare_centroids(0)
 
@@ -60,7 +65,7 @@ def tile_losskmeans_kernel(tc, base, x, cent, offs, out):
         x2_psum = psum.tile([P, N], F32, name="x2_psum")
         for c in range(D_CHUNKS):
             nc.vector.tensor_tensor(x_squared[:, c, :], x_sb[:, c, :], x_sb[:, c, :], MULT)
-            nc.tensor.matmul(x2_psum[:], ones[:, :P], x_squared[:, c, :], start=(c == 0), stop=(c == D_CHUNKS - 1))
+            nc.tensor.matmul(x2_psum[:], ones[:], x_squared[:, c, :], start=(c == 0), stop=(c == D_CHUNKS - 1))
         x2_rows = held.tile([P, N], F32, name="x2_rows")
         nc.vector.tensor_copy(x2_rows[:], x2_psum[:])
 

@@ -5,6 +5,8 @@ P = 128
 K, S, N, D = 512, 1024, 512, 256
 K_BLOCKS = K // P
 D_CHUNKS = D // P
+HALVES = 2
+H = N // HALVES
 
 FLOPS = 2 * K * N * D
 
@@ -43,7 +45,7 @@ def tile_losskmeans_kernel(tc, base, x, cent, offs, out):
         identity = held.tile([P, P], BF16, name="identity")
         make_identity(nc, identity[:])
 
-        warm_psum = psum.tile([P, N], F32, name="warm_psum")
+        warm_psum = psum.tile([P, N], F32, name="warm_psum", bufs=1)
         for i in range(WARM_MATMULS):
             nc.tensor.matmul(warm_psum[:], ones[:], ones[:, 0:1].to_broadcast([P, N]), start=True, stop=True)
 
@@ -62,7 +64,7 @@ def tile_losskmeans_kernel(tc, base, x, cent, offs, out):
         prepare_centroids(0)
 
         x_squared = held.tile([P, D_CHUNKS, N], BF16, name="x_squared")
-        x2_psum = psum.tile([P, N], F32, name="x2_psum")
+        x2_psum = psum.tile([P, N], F32, name="x2_psum", bufs=1)
         for c in range(D_CHUNKS):
             nc.vector.tensor_tensor(x_squared[:, c, :], x_sb[:, c, :], x_sb[:, c, :], MULT)
             nc.tensor.matmul(x2_psum[:], ones[:], x_squared[:, c, :], start=(c == 0), stop=(c == D_CHUNKS - 1))
@@ -70,12 +72,16 @@ def tile_losskmeans_kernel(tc, base, x, cent, offs, out):
         nc.vector.tensor_copy(x2_rows[:], x2_psum[:])
 
         for b in range(K_BLOCKS):
-            xc_psum = psum.tile([P, N], F32, name="xc_psum")
-            for c in range(D_CHUNKS):
-                nc.tensor.matmul(xc_psum[:], centT[b][:, c, :], x_sb[:, c, :], start=(c == 0), stop=(c == D_CHUNKS - 1))
-
             c2_minus_2xc = work.tile([P, N], F32, name="c2_minus_2xc")
-            nc.scalar.activation(c2_minus_2xc[:], xc_psum[:], ACT.Identity, bias=c2[:, b : b + 1], scale=-2.0)
+            for h in range(HALVES):
+                xc_psum = psum.tile([P, H], F32, name="xc_psum", bufs=2 * HALVES)
+                for c in range(D_CHUNKS):
+                    nc.tensor.matmul(
+                        xc_psum[:], centT[b][:, c, :], x_sb[:, c, h * H : (h + 1) * H], start=(c == 0), stop=(c == D_CHUNKS - 1)
+                    )
+                nc.scalar.activation(
+                    c2_minus_2xc[:, h * H : (h + 1) * H], xc_psum[:], ACT.Identity, bias=c2[:, b : b + 1], scale=-2.0
+                )
 
             if b + 1 < K_BLOCKS:
                 prepare_centroids(b + 1)

@@ -10,7 +10,7 @@ H = N // HALVES
 
 FLOPS = 2 * K * N * D
 
-WARM_MATMULS = 4
+WARM_MATMULS = 3
 
 BF16, F32, U16 = mybir.dt.bfloat16, mybir.dt.float32, mybir.dt.uint16
 ADD, MULT = mybir.AluOpType.add, mybir.AluOpType.mult

@@ -5,8 +5,8 @@ P = 128
 K, S, N, D = 512, 1024, 512, 256
 K_BLOCKS = K // P
 D_CHUNKS = D // P
-HALVES = 2
-H = N // HALVES
+PIECES = 4
+H = N // PIECES
 
 FLOPS = 2 * K * N * D
 
@@ -73,8 +73,8 @@ def tile_losskmeans_kernel(tc, base, x, cent, offs, out):
 
         for b in range(K_BLOCKS):
             c2_minus_2xc = work.tile([P, N], F32, name="c2_minus_2xc")
-            for h in range(HALVES):
-                xc_psum = psum.tile([P, H], F32, name="xc_psum", bufs=2 * HALVES)
+            for h in range(PIECES):
+                xc_psum = psum.tile([P, H], F32, name="xc_psum", bufs=PIECES)
                 for c in range(D_CHUNKS):
                     nc.tensor.matmul(
                         xc_psum[:], centT[b][:, c, :], x_sb[:, c, h * H : (h + 1) * H], start=(c == 0), stop=(c == D_CHUNKS - 1)

@@ -25,9 +25,9 @@ def tile_losskmeans_kernel(tc, base, x, cent, offs, out):
         tc.psum_pool(name="psum", bufs=2) as psum,
     ):
         cent_first = held.tile([P, D], BF16, name="cent_first")
-        nc.scalar.dma_start(cent_first[:], cent[0:P, :])
+        nc.sync.dma_start(cent_first[:], cent[0:P, :])
         x_sb = held.tile([P, D_CHUNKS, N], BF16, name="x_sb")
-        nc.sync.dma_start(x_sb[:], x.rearrange("(c p) n -> p c n", p=P))
+        nc.scalar.dma_start(x_sb[:], x.rearrange("(c p) n -> p c n", p=P))
         offsets = held.tile([P, N // 16], U16, name="offsets")
         nc.sync.dma_start(offsets[:], offs)
         windows = []

@@ -1,8 +1,8 @@
 import concourse.mybir as mybir
-from concourse.masks import make_identity
 
 P = 128
 K, S, N, D = 512, 1024, 512, 256
+Q = 32
 K_BLOCKS = K // P
 D_CHUNKS = D // P
 PIECES = 4
@@ -13,7 +13,7 @@ FLOPS = 2 * K * N * D
 WARM_MATMULS = 3
 
 BF16, F32, U16 = mybir.dt.bfloat16, mybir.dt.float32, mybir.dt.uint16
-ADD, MULT = mybir.AluOpType.add, mybir.AluOpType.mult
+ADD, MULT, IS_EQUAL = mybir.AluOpType.add, mybir.AluOpType.mult, mybir.AluOpType.is_equal
 ACT = mybir.ActivationFunctionType
 
 
@@ -34,16 +34,25 @@ def tile_losskmeans_kernel(tc, base, x, cent, offs, out):
         for b in range(K_BLOCKS):
             windows.append(held.tile([P, S], F32, name=f"window{b}"))
         nc.sync.dma_start(windows[0][:], base[0:P, :])
+        nc.sync.dma_start(windows[1][:], base[P : 2 * P, :])
         cent_rest = held.tile([P, K_BLOCKS - 1, D], BF16, name="cent_rest")
-        nc.scalar.dma_start(cent_rest[:], cent[P:K, :].rearrange("(b p) d -> p b d", p=P))
-        for b in range(1, K_BLOCKS):
+        nc.sync.dma_start(cent_rest[:], cent[P:K, :].rearrange("(b p) d -> p b d", p=P))
+        for b in range(2, K_BLOCKS):
             nc.sync.dma_start(windows[b][:], base[b * P : (b + 1) * P, :])
         cent_sb = [cent_first[:]] + [cent_rest[:, b - 1, :] for b in range(1, K_BLOCKS)]
 
         ones = held.tile([P, P], BF16, name="ones")
         nc.vector.memset(ones[:], 1.0)
         identity = held.tile([P, P], BF16, name="identity")
-        make_identity(nc, identity[:])
+        nc.vector.memset(identity[:], 0.0)
+        ramp_ones = held.tile([P, Q], F32, name="ramp_ones")
+        nc.vector.memset(ramp_ones[:], 1.0)
+        ramp = held.tile([P, Q], F32, name="ramp", align_bytes=64)
+        nc.vector.tensor_tensor_scan(ramp[:], ramp_ones[:], ramp_ones[:], 0.0, MULT, ADD)
+        ramp_turned = held.tile([P, Q], F32, name="ramp_turned", align_bytes=64)
+        nc.vector.transpose(ramp_turned[:], ramp[:])
+        for q in range(0, P, Q):
+            nc.vector.tensor_tensor(identity[q : q + Q, q : q + Q], ramp[q : q + Q, :], ramp_turned[q : q + Q, :], IS_EQUAL)
 
         warm_psum = psum.tile([P, N], F32, name="warm_psum", bufs=1)
         for i in range(WARM_MATMULS):

@@ -27,7 +27,7 @@ def tile_losskmeans_kernel(tc, base, x, cent, offs, out):
         cent_first = held.tile([P, D], BF16, name="cent_first")
         nc.sync.dma_start(cent_first[:], cent[0:P, :])
         x_sb = held.tile([P, D_CHUNKS, N], BF16, name="x_sb")
-        nc.scalar.dma_start(x_sb[:], x.rearrange("(c p) n -> p c n", p=P))
+        nc.sync.dma_start(x_sb[:], x.rearrange("(c p) n -> p c n", p=P))
         offsets = held.tile([P, N // 16], U16, name="offsets")
         nc.sync.dma_start(offsets[:], offs)
         windows = []

@@ -96,4 +96,8 @@ def tile_losskmeans_kernel(tc, base, x, cent, offs, out):
                 prepare_centroids(b + 1)
 
             nc.vector.tensor_tensor(windows[b][:].indirect(offsets[:]), c2_minus_2xc[:], x2_rows[:], ADD)
-            nc.sync.dma_start(out[b * P : (b + 1) * P, :], windows[b][:])
+            if b + 1 < K_BLOCKS:
+                nc.sync.dma_start(out[b * P : (b + 1) * P, :], windows[b][:])
+            else:
+                nc.sync.dma_start(out[b * P : (b + 1) * P, 0 : S // 2], windows[b][:, 0 : S // 2])
+                nc.scalar.dma_start(out[b * P : (b + 1) * P, S // 2 : S], windows[b][:, S // 2 : S])

@@ -72,6 +72,10 @@ def tile_losskmeans_kernel(tc, base, x, cent, offs, out):
 
         prepare_centroids(0)
 
+        nc.tensor.matmul(
+            warm_psum[:], ones[:], cent_first[:].unsqueeze(1).to_broadcast([P, N // D, D]), start=True, stop=True
+        )
+
         x_squared = held.tile([P, D_CHUNKS, N], BF16, name="x_squared")
         x2_psum = psum.tile([P, N], F32, name="x2_psum", bufs=1)
         for c in range(D_CHUNKS):

@@ -62,11 +62,11 @@ def tile_losskmeans_kernel(tc, base, x, cent, offs, out):
         centT = []
 
         def prepare_centroids(b):
-            centT_psum = psum.tile([P, D_CHUNKS, P], BF16, name="centT_psum")
-            for c in range(D_CHUNKS):
-                nc.tensor.transpose(centT_psum[:, c, :], cent_sb[b][:, c * P : (c + 1) * P], identity[:])
             centT.append(held.tile([P, D_CHUNKS, P], BF16, name=f"centT{b}"))
-            nc.scalar.activation(centT[b][:], centT_psum[:], ACT.Copy)
+            for c in range(D_CHUNKS):
+                centT_psum = psum.tile([P, P], BF16, name="centT_psum")
+                nc.tensor.transpose(centT_psum[:], cent_sb[b][:, c * P : (c + 1) * P], identity[:])
+                nc.scalar.activation(centT[b][:, c, :], centT_psum[:], ACT.Copy)
             cent_squared = work.tile([P, D], F32, name="cent_squared")
             nc.scalar.activation(cent_squared[:], cent_sb[b], ACT.Square, accum_out=c2[:, b : b + 1])
 

@@ -27,7 +27,7 @@ def tile_losskmeans_kernel(tc, base, x, cent, offs, out):
         cent_first = held.tile([P, D], BF16, name="cent_first")
         nc.sync.dma_start(cent_first[:], cent[0:P, :])
         x_sb = held.tile([P, D_CHUNKS, N], BF16, name="x_sb")
-        nc.sync.dma_start(x_sb[:], x.rearrange("(c p) n -> p c n", p=P))
+        nc.sync.dma_start(x_sb[:], x.rearrange("(p c) n -> p c n", p=P))
         offsets = held.tile([P, N // 16], U16, name="offsets")
         nc.sync.dma_start(offsets[:], offs)
         windows = []
@@ -65,7 +65,7 @@ def tile_losskmeans_kernel(tc, base, x, cent, offs, out):
             centT.append(held.tile([P, D_CHUNKS, P], BF16, name=f"centT{b}"))
             for c in range(D_CHUNKS):
                 centT_psum = psum.tile([P, P], BF16, name="centT_psum")
-                nc.tensor.transpose(centT_psum[:], cent_sb[b][:, c * P : (c + 1) * P], identity[:])
+                nc.tensor.transpose(centT_psum[:], cent_sb[b][:, c::D_CHUNKS], identity[:])
                 nc.scalar.activation(centT[b][:, c, :], centT_psum[:], ACT.Copy)
             cent_squared = work.tile([P, D], F32, name="cent_squared")
             nc.scalar.activation(cent_squared[:], cent_sb[b], ACT.Square, accum_out=c2[:, b : b + 1])

import concourse.mybir as mybir

P = 128
K, S, N, D = 512, 1024, 512, 256
Q = 32
K_BLOCKS = K // P
D_CHUNKS = D // P
PIECES = 4
H = N // PIECES

FLOPS = 2 * K * N * D

WARM_MATMULS = 3

BF16, F32, U16 = mybir.dt.bfloat16, mybir.dt.float32, mybir.dt.uint16
ADD, MULT, IS_EQUAL = mybir.AluOpType.add, mybir.AluOpType.mult, mybir.AluOpType.is_equal
ACT = mybir.ActivationFunctionType


def tile_losskmeans_kernel(tc, base, x, cent, offs, out):
    nc = tc.nc
    with (
        tc.tile_pool(name="held", bufs=1) as held,
        tc.tile_pool(name="work", bufs=2) as work,
        tc.psum_pool(name="psum", bufs=2) as psum,
    ):
        cent_first = held.tile([P, D], BF16, name="cent_first")
        nc.sync.dma_start(cent_first[:], cent[0:P, :])
        x_sb = held.tile([P, D_CHUNKS, N], BF16, name="x_sb")
        nc.sync.dma_start(x_sb[:], x.rearrange("(p c) n -> p c n", p=P))
        offsets = held.tile([P, N // 16], U16, name="offsets")
        nc.sync.dma_start(offsets[:], offs)
        windows = []
        for b in range(K_BLOCKS):
            windows.append(held.tile([P, S], F32, name=f"window{b}"))
        nc.sync.dma_start(windows[0][:], base[0:P, :])
        nc.sync.dma_start(windows[1][:], base[P : 2 * P, :])
        cent_rest = held.tile([P, K_BLOCKS - 1, D], BF16, name="cent_rest")
        nc.sync.dma_start(cent_rest[:], cent[P:K, :].rearrange("(b p) d -> p b d", p=P))
        for b in range(2, K_BLOCKS):
            nc.sync.dma_start(windows[b][:], base[b * P : (b + 1) * P, :])
        cent_sb = [cent_first[:]] + [cent_rest[:, b - 1, :] for b in range(1, K_BLOCKS)]

        ones = held.tile([P, P], BF16, name="ones")
        nc.vector.memset(ones[:], 1.0)
        identity = held.tile([P, P], BF16, name="identity")
        nc.vector.memset(identity[:], 0.0)
        ramp_ones = held.tile([P, Q], F32, name="ramp_ones")
        nc.vector.memset(ramp_ones[:], 1.0)
        ramp = held.tile([P, Q], F32, name="ramp", align_bytes=64)
        nc.vector.tensor_tensor_scan(ramp[:], ramp_ones[:], ramp_ones[:], 0.0, MULT, ADD)
        ramp_turned = held.tile([P, Q], F32, name="ramp_turned", align_bytes=64)
        nc.vector.transpose(ramp_turned[:], ramp[:])
        for q in range(0, P, Q):
            nc.vector.tensor_tensor(identity[q : q + Q, q : q + Q], ramp[q : q + Q, :], ramp_turned[q : q + Q, :], IS_EQUAL)

        warm_psum = psum.tile([P, N], F32, name="warm_psum", bufs=1)
        for i in range(WARM_MATMULS):
            nc.tensor.matmul(warm_psum[:], ones[:], ones[:, 0:1].to_broadcast([P, N]), start=True, stop=True)

        c2 = held.tile([P, K_BLOCKS], F32, name="c2")
        centT = []

        def prepare_centroids(b):
            centT.append(held.tile([P, D_CHUNKS, P], BF16, name=f"centT{b}"))
            for c in range(D_CHUNKS):
                centT_psum = psum.tile([P, P], BF16, name="centT_psum")
                nc.tensor.transpose(centT_psum[:], cent_sb[b][:, c::D_CHUNKS], identity[:])
                nc.scalar.activation(centT[b][:, c, :], centT_psum[:], ACT.Copy)
            cent_squared = work.tile([P, D], F32, name="cent_squared")
            nc.scalar.activation(cent_squared[:], cent_sb[b], ACT.Square, accum_out=c2[:, b : b + 1])

        prepare_centroids(0)

        nc.tensor.matmul(
            warm_psum[:], ones[:], cent_first[:].unsqueeze(1).to_broadcast([P, N // D, D]), start=True, stop=True
        )

        x_squared = held.tile([P, D_CHUNKS, N], BF16, name="x_squared")
        x2_psum = psum.tile([P, N], F32, name="x2_psum", bufs=1)
        for c in range(D_CHUNKS):
            nc.vector.tensor_tensor(x_squared[:, c, :], x_sb[:, c, :], x_sb[:, c, :], MULT)
            nc.tensor.matmul(x2_psum[:], ones[:], x_squared[:, c, :], start=(c == 0), stop=(c == D_CHUNKS - 1))
        x2_rows = held.tile([P, N], F32, name="x2_rows")
        nc.vector.tensor_copy(x2_rows[:], x2_psum[:])

        for b in range(K_BLOCKS):
            c2_minus_2xc = work.tile([P, N], F32, name="c2_minus_2xc")
            for h in range(PIECES):
                xc_psum = psum.tile([P, H], F32, name="xc_psum", bufs=PIECES)
                for c in range(D_CHUNKS):
                    nc.tensor.matmul(
                        xc_psum[:], centT[b][:, c, :], x_sb[:, c, h * H : (h + 1) * H], start=(c == 0), stop=(c == D_CHUNKS - 1)
                    )
                nc.scalar.activation(
                    c2_minus_2xc[:, h * H : (h + 1) * H], xc_psum[:], ACT.Identity, bias=c2[:, b : b + 1], scale=-2.0
                )

            if b + 1 < K_BLOCKS:
                prepare_centroids(b + 1)

            nc.vector.tensor_tensor(windows[b][:].indirect(offsets[:]), c2_minus_2xc[:], x2_rows[:], ADD)
            if b + 1 < K_BLOCKS:
                nc.sync.dma_start(out[b * P : (b + 1) * P, :], windows[b][:])
            else:
                nc.sync.dma_start(out[b * P : (b + 1) * P, 0 : S // 2], windows[b][:, 0 : S // 2])
                nc.scalar.dma_start(out[b * P : (b + 1) * P, S // 2 : S], windows[b][:, S // 2 : S])
